import numpy as np
import ml_dtypes


def mxq(x, axis, fmt="e4m3"):
    dtype, down = {"e4m3": (ml_dtypes.float8_e4m3fn, 7), "e5m2": (ml_dtypes.float8_e5m2, 14)}[fmt]
    v = np.moveaxis(np.asarray(x, np.float32).astype(ml_dtypes.bfloat16).astype(np.float64), axis, -1)
    blocks = v.reshape(v.shape[:-1] + (-1, 32))
    amax = np.abs(blocks).max(-1, keepdims=True)
    byte = np.maximum(np.where(amax > 0, np.frexp(amax)[1] - 1 + 127, 0) - down, 1)
    scale = np.exp2(byte - 127.0)
    codes = (blocks / scale).astype(np.float32).astype(dtype).astype(np.float64)
    return np.moveaxis((codes * scale).reshape(v.shape), -1, axis)


WIDE = False


def mx_kscale(k):
    if not WIDE:
        return np.ones(k)
    levels = np.array([10, -10, 5, -5, 0])
    a = np.random.permutation(np.resize(levels, k // 512 * 4)).reshape(k // 512, 4)
    idx = np.arange(k)
    return np.exp2(a[idx // 512, idx % 128 // 32])


BF16 = ml_dtypes.bfloat16


def bf(x):
    return np.asarray(x, np.float32).astype(BF16)


def f64(x):
    return np.asarray(x).astype(np.float64)


B, S, D, E, R = 2, 256, 16384, 8, 64


def setup_inputs():
    s = mx_kscale(D)
    return {"x": bf(np.random.standard_normal((B, S, D)) * s),
            "W": bf(np.random.standard_normal((E, R, D)) * (1.0 / np.sqrt(D)) / s)}


def reference(x, W):
    xq = mxq(f64(x), 2, "e4m3")
    Wq = mxq(f64(W), 2, "e4m3")
    y = xq[None, :, :, :] @ Wq.transpose(0, 2, 1)[:, None, :, :]
    return tuple(y[e] for e in range(W.shape[0]))

@@ -1,0 +1,129 @@
+from contextlib import ExitStack
+
+import concourse.mybir as mybir
+from concourse.masks import make_identity
+
+BF16 = mybir.dt.bfloat16
+F32 = mybir.dt.float32
+U32 = mybir.dt.uint32
+U8 = mybir.dt.uint8
+FP8X4 = mybir.dt.float8_e4m3fn_x4
+
+P = 128
+D = 16384
+ROWS = 512
+EXPERTS = 8
+RANK = 64
+ROW_TILES = ROWS // P
+
+D_PASS = 4 * P
+PASSES = D // D_PASS
+WORDS_PASS = D_PASS // 2
+BANK_WORDS = 512
+BANKS_PASS = 2 * ROWS * WORDS_PASS // (P * BANK_WORDS)
+
+PASSES_PER_LOAD = 4
+LOAD_COLS = PASSES_PER_LOAD * D_PASS
+LOADS = PASSES // PASSES_PER_LOAD
+LOADS_AHEAD = 3
+
+PASSES_PER_ROUND = 1
+
+FLOPS = 2 * ROWS * ROWS * D
+
+
+def tile_moelineara_k_kernel(tc, x, W, *outs):
+    nc = tc.nc
+
+    x_rows = x.flatten_outer_dims().rearrange("(p i) d -> p i d", i=ROW_TILES)
+    w_rows = W.flatten_outer_dims().rearrange("(j p) d -> p j d", p=P)
+
+    with ExitStack() as ctx:
+        ctx.enter_context(tc.manual_schedule())
+        fixed = ctx.enter_context(tc.tile_pool(name="fixed", bufs=1))
+        stage = ctx.enter_context(tc.tile_pool(name="stage", bufs=LOADS_AHEAD + 1))
+        group = ctx.enter_context(tc.tile_pool(name="group", bufs=3))
+        quant = ctx.enter_context(tc.tile_pool(name="quant", bufs=2 * PASSES_PER_ROUND + 1))
+        turned = ctx.enter_context(tc.psum_pool(name="turned", bufs=BANKS_PASS))
+        sums = ctx.enter_context(tc.psum_pool(name="sums", bufs=1))
+
+        ident = fixed.tile([P, P], F32, name="ident")
+        make_identity(nc, ident[:])
+
+        acc = [sums.tile([P, ROWS], F32, name="acc%d" % i) for i in range(ROW_TILES)]
+
+        def load(step):
+            x_stage = stage.tile([P, ROW_TILES, LOAD_COLS], BF16, name="x_stage")
+            w_stage = stage.tile([P, ROW_TILES, LOAD_COLS], BF16, name="w_stage")
+            pieces = PASSES_PER_LOAD if step == 0 else 1
+            width = LOAD_COLS // pieces
+            for piece in range(pieces):
+                here = slice(piece * width, (piece + 1) * width)
+                there = slice(step * LOAD_COLS + piece * width, step * LOAD_COLS + (piece + 1) * width)
+                nc.sync.dma_start(out=x_stage[:, :, here], in_=x_rows[:, :, there])
+                nc.sync.dma_start(out=w_stage[:, :, here], in_=w_rows[:, :, there])
+            return x_stage, w_stage
+
+        def turn_and_quantise(staged, c):
+            grouped = group.tile([P, 2 * ROWS * 4], BF16, name="grouped", align_bytes=64)
+            grouped_words = grouped[:].bitcast(F32)
+            for b in range(BANKS_PASS):
+                operand = staged[b // 2]
+                bank = turned.tile([P, 2, 2 * P], F32, name="bank")
+                for j in range(2):
+                    words = operand[:, 2 * (b % 2) + j, :].bitcast(F32)
+                    for u in range(2):
+                        first = WORDS_PASS * c + P * u
+                        nc.tensor.transpose(
+                            bank[:, u, P * j : P * (j + 1)], words[:, first : first + P], ident[:]
+                        )
+                copy = nc.vector.tensor_copy if b == BANKS_PASS - 1 else nc.scalar.copy
+                copy(
+                    out=grouped_words[:, BANK_WORDS * b : BANK_WORDS * (b + 1)].rearrange(
+                        "p (c u) -> p c u", u=2
+                    ),
+                    in_=bank[:].rearrange("p u c -> p c u"),
+                )
+            codes = quant.tile([P, 2 * ROWS], U32, name="codes", align_bytes=64)
+            scales = quant.tile([P, 2 * ROWS], U8, name="scales", align_bytes=64)
+            nc.vector.quantize_mx(out=codes[:].bitcast(FP8X4), scales=scales[:], in_=grouped[:])
+            return codes, scales
+
+        def multiply(g, codes, scales):
+            for i in range(ROW_TILES):
+                tokens = slice(P * i, P * (i + 1))
+                nc.tensor.matmul_mx(
+                    out=acc[i][:],
+                    lhsT=codes[:, tokens].bitcast(FP8X4),
+                    lhsT_scale=scales[:, tokens],
+                    rhs=codes[:, ROWS : 2 * ROWS].bitcast(FP8X4),
+                    rhs_scale=scales[:, ROWS : 2 * ROWS],
+                    start=(g == 0),
+                    stop=(g == PASSES - 1),
+                )
+
+        staged = [load(step) for step in range(LOADS_AHEAD)]
+        ready = []
+        for first_pass in range(0, PASSES, PASSES_PER_ROUND):
+            fresh = []
+            for g in range(first_pass, first_pass + PASSES_PER_ROUND):
+                step, c = divmod(g, PASSES_PER_LOAD)
+                if c == 0 and step + LOADS_AHEAD < LOADS:
+                    staged.append(load(step + LOADS_AHEAD))
+                codes, scales = turn_and_quantise(staged[step], c)
+                fresh.append((g, codes, scales))
+            for g, codes, scales in ready:
+                multiply(g, codes, scales)
+            ready = fresh
+        for g, codes, scales in ready:
+            multiply(g, codes, scales)
+
+        result = fixed.tile([P, EXPERTS, ROW_TILES, RANK], F32, name="result")
+        for i in range(ROW_TILES):
+            copy = nc.scalar.copy if i % 2 == 0 else nc.vector.tensor_copy
+            copy(out=result[:, :, i, :], in_=acc[i][:].rearrange("p (e r) -> p e r", e=EXPERTS))
+        for e in range(EXPERTS):
+            nc.sync.dma_start(
+                out=outs[e].flatten_outer_dims().rearrange("(p i) r -> p i r", i=ROW_TILES),
+                in_=result[:, e, :, :],
+            )

@@ -22,12 +22,13 @@ WORDS_PASS = D_PASS // 2
 BANK_WORDS = 512
 BANKS_PASS = 2 * ROWS * WORDS_PASS // (P * BANK_WORDS)
 
-PASSES_PER_LOAD = 4
-LOAD_COLS = PASSES_PER_LOAD * D_PASS
-LOADS = PASSES // PASSES_PER_LOAD
-LOADS_AHEAD = 3
+HEAD_PASSES = 8
+PASSES_PER_LOAD = 2
+LOADS_AHEAD = 7
 
 PASSES_PER_ROUND = 1
+ROUNDS = PASSES // PASSES_PER_ROUND
+LAG = 1
 
 FLOPS = 2 * ROWS * ROWS * D
 
@@ -43,7 +44,7 @@ def tile_moelineara_k_kernel(tc, x, W, *outs):
         fixed = ctx.enter_context(tc.tile_pool(name="fixed", bufs=1))
         stage = ctx.enter_context(tc.tile_pool(name="stage", bufs=LOADS_AHEAD + 1))
         group = ctx.enter_context(tc.tile_pool(name="group", bufs=3))
-        quant = ctx.enter_context(tc.tile_pool(name="quant", bufs=2 * PASSES_PER_ROUND + 1))
+        quant = ctx.enter_context(tc.tile_pool(name="quant", bufs=(LAG + 1) * PASSES_PER_ROUND + 1))
         turned = ctx.enter_context(tc.psum_pool(name="turned", bufs=BANKS_PASS))
         sums = ctx.enter_context(tc.psum_pool(name="sums", bufs=1))
 
@@ -52,23 +53,19 @@ def tile_moelineara_k_kernel(tc, x, W, *outs):
 
         acc = [sums.tile([P, ROWS], F32, name="acc%d" % i) for i in range(ROW_TILES)]
 
-        def load(step):
-            x_stage = stage.tile([P, ROW_TILES, LOAD_COLS], BF16, name="x_stage")
-            w_stage = stage.tile([P, ROW_TILES, LOAD_COLS], BF16, name="w_stage")
-            pieces = PASSES_PER_LOAD if step == 0 else 1
-            width = LOAD_COLS // pieces
-            for piece in range(pieces):
-                here = slice(piece * width, (piece + 1) * width)
-                there = slice(step * LOAD_COLS + piece * width, step * LOAD_COLS + (piece + 1) * width)
-                nc.sync.dma_start(out=x_stage[:, :, here], in_=x_rows[:, :, there])
-                nc.sync.dma_start(out=w_stage[:, :, here], in_=w_rows[:, :, there])
+        def load(first_pass, count):
+            x_stage = stage.tile([P, ROW_TILES, PASSES_PER_LOAD * D_PASS], BF16, name="x_stage")
+            w_stage = stage.tile([P, ROW_TILES, PASSES_PER_LOAD * D_PASS], BF16, name="w_stage")
+            columns = slice(first_pass * D_PASS, (first_pass + count) * D_PASS)
+            nc.sync.dma_start(out=x_stage[:, :, : count * D_PASS], in_=x_rows[:, :, columns])
+            nc.sync.dma_start(out=w_stage[:, :, : count * D_PASS], in_=w_rows[:, :, columns])
             return x_stage, w_stage
 
-        def turn_and_quantise(staged, c):
+        def turn_and_quantise(pair, c):
             grouped = group.tile([P, 2 * ROWS * 4], BF16, name="grouped", align_bytes=64)
             grouped_words = grouped[:].bitcast(F32)
             for b in range(BANKS_PASS):
-                operand = staged[b // 2]
+                operand = pair[b // 2]
                 bank = turned.tile([P, 2, 2 * P], F32, name="bank")
                 for j in range(2):
                     words = operand[:, 2 * (b % 2) + j, :].bitcast(F32)
@@ -102,21 +99,23 @@ def tile_moelineara_k_kernel(tc, x, W, *outs):
                     stop=(g == PASSES - 1),
                 )
 
-        staged = [load(step) for step in range(LOADS_AHEAD)]
-        ready = []
-        for first_pass in range(0, PASSES, PASSES_PER_ROUND):
-            fresh = []
-            for g in range(first_pass, first_pass + PASSES_PER_ROUND):
-                step, c = divmod(g, PASSES_PER_LOAD)
-                if c == 0 and step + LOADS_AHEAD < LOADS:
-                    staged.append(load(step + LOADS_AHEAD))
-                codes, scales = turn_and_quantise(staged[step], c)
-                fresh.append((g, codes, scales))
-            for g, codes, scales in ready:
-                multiply(g, codes, scales)
-            ready = fresh
-        for g, codes, scales in ready:
-            multiply(g, codes, scales)
+        loads = [(g, 1) for g in range(HEAD_PASSES)]
+        loads.extend([(g, PASSES_PER_LOAD) for g in range(HEAD_PASSES, PASSES, PASSES_PER_LOAD)])
+        home = [(n, c) for n, (first_pass, count) in enumerate(loads) for c in range(count)]
+
+        staged = []
+        quantised = []
+        for round_no in range(ROUNDS + LAG):
+            if round_no < ROUNDS:
+                for g in range(round_no * PASSES_PER_ROUND, (round_no + 1) * PASSES_PER_ROUND):
+                    n, c = home[g]
+                    for ahead in range(len(staged), min(n + LOADS_AHEAD + 1, len(loads))):
+                        staged.append(load(loads[ahead][0], loads[ahead][1]))
+                    quantised.append(turn_and_quantise(staged[n], c))
+            if round_no >= LAG:
+                late = round_no - LAG
+                for g in range(late * PASSES_PER_ROUND, (late + 1) * PASSES_PER_ROUND):
+                    multiply(g, quantised[g][0], quantised[g][1])
 
         result = fixed.tile([P, EXPERTS, ROW_TILES, RANK], F32, name="result")
         for i in range(ROW_TILES):

@@ -28,7 +28,7 @@ LOADS_AHEAD = 7
 
 PASSES_PER_ROUND = 1
 ROUNDS = PASSES // PASSES_PER_ROUND
-LAG = 1
+LAG = 2
 
 FLOPS = 2 * ROWS * ROWS * D
 

@@ -26,9 +26,9 @@ HEAD_PASSES = 8
 PASSES_PER_LOAD = 2
 LOADS_AHEAD = 7
 
-PASSES_PER_ROUND = 1
+PASSES_PER_ROUND = 2
 ROUNDS = PASSES // PASSES_PER_ROUND
-LAG = 2
+LAG = 1
 
 FLOPS = 2 * ROWS * ROWS * D
 

from contextlib import ExitStack

import concourse.mybir as mybir
from concourse.masks import make_identity

BF16 = mybir.dt.bfloat16
F32 = mybir.dt.float32
U32 = mybir.dt.uint32
U8 = mybir.dt.uint8
FP8X4 = mybir.dt.float8_e4m3fn_x4

P = 128
D = 16384
ROWS = 512
EXPERTS = 8
RANK = 64
ROW_TILES = ROWS // P

D_PASS = 4 * P
PASSES = D // D_PASS
WORDS_PASS = D_PASS // 2
BANK_WORDS = 512
BANKS_PASS = 2 * ROWS * WORDS_PASS // (P * BANK_WORDS)

HEAD_PASSES = 8
PASSES_PER_LOAD = 2
LOADS_AHEAD = 7

PASSES_PER_ROUND = 2
ROUNDS = PASSES // PASSES_PER_ROUND
LAG = 1

FLOPS = 2 * ROWS * ROWS * D


def tile_moelineara_k_kernel(tc, x, W, *outs):
    nc = tc.nc

    x_rows = x.flatten_outer_dims().rearrange("(p i) d -> p i d", i=ROW_TILES)
    w_rows = W.flatten_outer_dims().rearrange("(j p) d -> p j d", p=P)

    with ExitStack() as ctx:
        ctx.enter_context(tc.manual_schedule())
        fixed = ctx.enter_context(tc.tile_pool(name="fixed", bufs=1))
        stage = ctx.enter_context(tc.tile_pool(name="stage", bufs=LOADS_AHEAD + 1))
        group = ctx.enter_context(tc.tile_pool(name="group", bufs=3))
        quant = ctx.enter_context(tc.tile_pool(name="quant", bufs=(LAG + 1) * PASSES_PER_ROUND + 1))
        turned = ctx.enter_context(tc.psum_pool(name="turned", bufs=BANKS_PASS))
        sums = ctx.enter_context(tc.psum_pool(name="sums", bufs=1))

        ident = fixed.tile([P, P], F32, name="ident")
        make_identity(nc, ident[:])

        acc = [sums.tile([P, ROWS], F32, name="acc%d" % i) for i in range(ROW_TILES)]

        def load(first_pass, count):
            x_stage = stage.tile([P, ROW_TILES, PASSES_PER_LOAD * D_PASS], BF16, name="x_stage")
            w_stage = stage.tile([P, ROW_TILES, PASSES_PER_LOAD * D_PASS], BF16, name="w_stage")
            columns = slice(first_pass * D_PASS, (first_pass + count) * D_PASS)
            nc.sync.dma_start(out=x_stage[:, :, : count * D_PASS], in_=x_rows[:, :, columns])
            nc.sync.dma_start(out=w_stage[:, :, : count * D_PASS], in_=w_rows[:, :, columns])
            return x_stage, w_stage

        def turn_and_quantise(pair, c):
            grouped = group.tile([P, 2 * ROWS * 4], BF16, name="grouped", align_bytes=64)
            grouped_words = grouped[:].bitcast(F32)
            for b in range(BANKS_PASS):
                operand = pair[b // 2]
                bank = turned.tile([P, 2, 2 * P], F32, name="bank")
                for j in range(2):
                    words = operand[:, 2 * (b % 2) + j, :].bitcast(F32)
                    for u in range(2):
                        first = WORDS_PASS * c + P * u
                        nc.tensor.transpose(
                            bank[:, u, P * j : P * (j + 1)], words[:, first : first + P], ident[:]
                        )
                copy = nc.vector.tensor_copy if b == BANKS_PASS - 1 else nc.scalar.copy
                copy(
                    out=grouped_words[:, BANK_WORDS * b : BANK_WORDS * (b + 1)].rearrange(
                        "p (c u) -> p c u", u=2
                    ),
                    in_=bank[:].rearrange("p u c -> p c u"),
                )
            codes = quant.tile([P, 2 * ROWS], U32, name="codes", align_bytes=64)
            scales = quant.tile([P, 2 * ROWS], U8, name="scales", align_bytes=64)
            nc.vector.quantize_mx(out=codes[:].bitcast(FP8X4), scales=scales[:], in_=grouped[:])
            return codes, scales

        def multiply(g, codes, scales):
            for i in range(ROW_TILES):
                tokens = slice(P * i, P * (i + 1))
                nc.tensor.matmul_mx(
                    out=acc[i][:],
                    lhsT=codes[:, tokens].bitcast(FP8X4),
                    lhsT_scale=scales[:, tokens],
                    rhs=codes[:, ROWS : 2 * ROWS].bitcast(FP8X4),
                    rhs_scale=scales[:, ROWS : 2 * ROWS],
                    start=(g == 0),
                    stop=(g == PASSES - 1),
                )

        loads = [(g, 1) for g in range(HEAD_PASSES)]
        loads.extend([(g, PASSES_PER_LOAD) for g in range(HEAD_PASSES, PASSES, PASSES_PER_LOAD)])
        home = [(n, c) for n, (first_pass, count) in enumerate(loads) for c in range(count)]

        staged = []
        quantised = []
        for round_no in range(ROUNDS + LAG):
            if round_no < ROUNDS:
                for g in range(round_no * PASSES_PER_ROUND, (round_no + 1) * PASSES_PER_ROUND):
                    n, c = home[g]
                    for ahead in range(len(staged), min(n + LOADS_AHEAD + 1, len(loads))):
                        staged.append(load(loads[ahead][0], loads[ahead][1]))
                    quantised.append(turn_and_quantise(staged[n], c))
            if round_no >= LAG:
                late = round_no - LAG
                for g in range(late * PASSES_PER_ROUND, (late + 1) * PASSES_PER_ROUND):
                    multiply(g, quantised[g][0], quantised[g][1])

        result = fixed.tile([P, EXPERTS, ROW_TILES, RANK], F32, name="result")
        for i in range(ROW_TILES):
            copy = nc.scalar.copy if i % 2 == 0 else nc.vector.tensor_copy
            copy(out=result[:, :, i, :], in_=acc[i][:].rearrange("p (e r) -> p e r", e=EXPERTS))
        for e in range(EXPERTS):
            nc.sync.dma_start(
                out=outs[e].flatten_outer_dims().rearrange("(p i) r -> p i r", i=ROW_TILES),
                in_=result[:, e, :, :],
            )
